import numpy as np
import ml_dtypes


def mxq(x, axis, fmt="e4m3"):
    dtype, down = {"e4m3": (ml_dtypes.float8_e4m3fn, 7), "e5m2": (ml_dtypes.float8_e5m2, 14)}[fmt]
    v = np.moveaxis(np.asarray(x, np.float32).astype(ml_dtypes.bfloat16).astype(np.float64), axis, -1)
    blocks = v.reshape(v.shape[:-1] + (-1, 32))
    amax = np.abs(blocks).max(-1, keepdims=True)
    byte = np.maximum(np.where(amax > 0, np.frexp(amax)[1] - 1 + 127, 0) - down, 1)
    scale = np.exp2(byte - 127.0)
    codes = (blocks / scale).astype(np.float32).astype(dtype).astype(np.float64)
    return np.moveaxis((codes * scale).reshape(v.shape), -1, axis)


WIDE = False


def mx_kscale(k):
    if not WIDE:
        return np.ones(k)
    levels = np.array([10, -10, 5, -5, 0])
    if k % 512:
        return np.exp2(np.random.permutation(np.resize(levels, k // 32))).repeat(32)
    a = np.empty((k // 512, 16))
    for p in range(k // 512):
        a[p, :8] = np.random.permutation(np.resize(levels, 8))
        for g in range(8):
            far = levels[np.abs(levels - a[p, g]) >= 10]
            a[p, g + 8] = far[np.random.randint(len(far))]
    return np.exp2(a.ravel()).repeat(32)


BF16 = ml_dtypes.bfloat16


def bf(x):
    return np.asarray(x, np.float32).astype(BF16)


def f64(x):
    return np.asarray(x).astype(np.float64)


B, T, DM, DH, L = 4, 512, 1024, 1024, 512


def sigmoid(x):
    return 1.0 / (1.0 + np.exp(-x))


def setup_inputs():
    s, t = mx_kscale(DM), mx_kscale(DH)
    return {"q": bf(np.random.standard_normal((B, T, DM)) * s),
            "num": bf(np.random.standard_normal((B, T, DH)) * 1.9 * np.sqrt(T) * t),
            "den": bf(0.5 * T * (0.5 + np.random.random((B, T, DH)))),
            "Wq": bf(np.random.standard_normal((DH, DM)) / np.sqrt(DM) / s),
            "Wo": bf(np.random.standard_normal((DM, DH)) * 5.0 / np.sqrt(DH) / t)}


def reference(q, num, den, Wq, Wo):
    Q = mxq(f64(q), 2, "e4m3") @ mxq(f64(Wq), 1, "e4m3").T
    Yt = sigmoid(Q) * f64(num) / f64(den)
    return mxq(Yt, 2, "e4m3") @ mxq(f64(Wo), 1, "e4m3").T

@@ -1,0 +1,242 @@
+from contextlib import ExitStack
+
+import concourse.mybir as mybir
+from concourse.masks import make_identity
+
+F32 = mybir.dt.float32
+BF16 = mybir.dt.bfloat16
+U32 = mybir.dt.uint32
+U8 = mybir.dt.uint8
+FP8X4 = mybir.dt.float8_e4m3fn_x4
+ACT = mybir.ActivationFunctionType
+MULT = mybir.AluOpType.mult
+
+P = 128
+PACK = 4
+K_PASS = P * PACK
+WIDTH = 1024
+PASSES = WIDTH // K_PASS
+BLOCK = 512
+PAIR = 2 * P
+HALVES = BLOCK // PAIR
+TOKENS = 2048
+CHUNKS = TOKENS // BLOCK
+UNITS = CHUNKS * PASSES
+EARLY_CHUNKS = 2
+PROJECT_BEHIND = 3
+RATIO_AHEAD = 7
+
+FLOPS = 2 * 2 * TOKENS * WIDTH * WIDTH
+
+
+def tile_aftfull_pb_kernel(tc, q, num, den, Wq, Wo, out):
+    nc = tc.nc
+
+    by_token = "(n p h j) k -> n h p (j k)"
+    q_rows = q.flatten_outer_dims().rearrange(by_token, p=P, h=HALVES, j=2).unsqueeze(3)
+    num_rows = num.flatten_outer_dims().rearrange(by_token, p=P, h=HALVES, j=2).unsqueeze(3)
+    den_rows = den.flatten_outer_dims().rearrange(by_token, p=P, h=HALVES, j=2).unsqueeze(3)
+    out_rows = out.flatten_outer_dims().rearrange("(n p i) o -> n p i o", p=P, i=2 * HALVES)
+    wq_rows = Wq.rearrange("(g p u e) k -> g u p (e k)", u=HALVES, p=P, e=2).unsqueeze(3)
+    wo_rows = Wo.rearrange("(s h j p) k -> s h p j k", h=HALVES, j=2, p=P)
+
+    with ExitStack() as ctx:
+        ctx.enter_context(tc.manual_schedule())
+        const = ctx.enter_context(tc.tile_pool(name="const", bufs=1))
+        nat_pool = ctx.enter_context(tc.tile_pool(name="nat", bufs=10))
+        grouped_pool = ctx.enter_context(tc.tile_pool(name="grouped", bufs=2))
+        keep = ctx.enter_context(tc.tile_pool(name="keep", bufs=1))
+        sig_pool = ctx.enter_context(tc.tile_pool(name="sig", bufs=3))
+        y_pool = ctx.enter_context(tc.tile_pool(name="y", bufs=2))
+        out_pool = ctx.enter_context(tc.tile_pool(name="outs", bufs=4))
+        for_scalar = ctx.enter_context(tc.psum_pool(name="for_scalar", bufs=4))
+        for_vector = ctx.enter_context(tc.psum_pool(name="for_vector", bufs=4))
+
+        ident = const.tile([P, P], F32, name="ident")
+        make_identity(nc, ident[:])
+
+        def load(rows):
+            nat = nat_pool.tile([P, 2, WIDTH], BF16, name="nat")
+            runs = rows.shape[1]
+            nc.sync.dma_start(out=nat[:].rearrange("p (a b) k -> p a (b k)", a=runs), in_=rows)
+            return nat
+
+        def load_block(rows):
+            return [load(rows[h]) for h in range(HALVES)]
+
+        def mx_tiles(name):
+            return {
+                "codes": keep.tile([P, PASSES * BLOCK], U32, name=name + "_codes", align_bytes=64),
+                "scales": keep.tile([P, PASSES * BLOCK], U8, name=name + "_scales", align_bytes=64),
+            }
+
+        def turn(nat, c, pool):
+            words = nat[:].bitcast(F32)
+            bank = pool.tile([P, 2, PAIR], F32, name="bank")
+            for u in range(2):
+                for j in range(2):
+                    first = 2 * c * P + u
+                    nc.tensor.transpose(
+                        out=bank[:, u, j * P : (j + 1) * P],
+                        in_=words[:, j, first : 2 * (c + 1) * P : 2],
+                        identity=ident[:],
+                    )
+            return bank
+
+        def as_values(bank):
+            return bank[:].bitcast(BF16).rearrange("p u (r e) -> p r u e", e=2)
+
+        def part_of(unit_tile, h):
+            rows = unit_tile[:, h * PAIR : (h + 1) * PAIR, :]
+            return rows.rearrange("p r (u e) -> p r u e", e=2)
+
+        def new_grouped():
+            return grouped_pool.tile([P, PASSES, BLOCK, PACK], BF16, name="grouped", align_bytes=64)
+
+        def regroup(nat, grouped, h, on_scalar):
+            banks = [turn(nat, c, for_scalar if on_scalar else for_vector) for c in range(PASSES)]
+            for c in range(PASSES):
+                side_by_side = grouped[:].bitcast(F32)[:, c, h * PAIR : (h + 1) * PAIR, :]
+                planes = banks[c][:].rearrange("p u r -> p r u")
+                if on_scalar:
+                    nc.scalar.copy(out=side_by_side, in_=planes)
+                else:
+                    nc.vector.tensor_copy(out=side_by_side, in_=planes)
+
+        def quantise(grouped, operand):
+            nc.vector.quantize_mx(
+                out=operand["codes"][:].bitcast(FP8X4),
+                scales=operand["scales"][:],
+                in_=grouped[:].rearrange("p c r t -> p (c r t)"),
+            )
+
+        def log_denominator(nat, n, h):
+            banks = [turn(nat, g, for_scalar) for g in range(PASSES)]
+            for g in range(PASSES):
+                nc.scalar.activation(
+                    out=part_of(ratio[PASSES * n + g], h), in_=as_values(banks[g]), func=ACT.Ln
+                )
+
+        def ratio_unit(u):
+            n, g = divmod(u, PASSES)
+            banks = [turn(num_nat[n][h], g, for_vector) for h in range(HALVES)]
+            for h in range(HALVES):
+                part = part_of(ratio[u], h)
+                nc.vector.tensor_tensor(out=part, in0=as_values(banks[h]), in1=part, op=MULT)
+
+        def mx_product(acc, stationary, s_col, moving):
+            for c in range(PASSES):
+                s_cols = slice(c * BLOCK + s_col, c * BLOCK + s_col + P)
+                m_cols = slice(c * BLOCK, (c + 1) * BLOCK)
+                nc.tensor.matmul_mx(
+                    out=acc[:],
+                    lhsT=stationary["codes"][:, s_cols].bitcast(FP8X4),
+                    lhsT_scale=stationary["scales"][:, s_cols],
+                    rhs=moving["codes"][:, m_cols].bitcast(FP8X4),
+                    rhs_scale=moving["scales"][:, m_cols],
+                    start=(c == 0),
+                    stop=(c == PASSES - 1),
+                )
+
+        def gate(u):
+            n, g = divmod(u, PASSES)
+            sig = sig_pool.tile([P, PACK, BLOCK], F32, name="sig")
+            for t in range(PACK):
+                acc = for_scalar.tile([P, BLOCK], F32, name="bank")
+                mx_product(acc, wq[g], t * P, qx[n])
+                nc.scalar.activation(out=sig[:, t, :], in_=acc[:], func=ACT.Sigmoid)
+            return sig
+
+        def blend(u, sig):
+            y = y_pool.tile([P, BLOCK, PACK], BF16, name="y", align_bytes=64)
+            nc.vector.tensor_tensor(out=y[:], in0=sig[:].rearrange("p t r -> p r t"), in1=ratio[u][:], op=MULT)
+            return y
+
+        def quantise_y(u, y):
+            n, g = divmod(u, PASSES)
+            cols = slice(g * BLOCK, (g + 1) * BLOCK)
+            nc.vector.quantize_mx(
+                out=yx[n]["codes"][:, cols].bitcast(FP8X4),
+                scales=yx[n]["scales"][:, cols],
+                in_=y[:].rearrange("p r t -> p (r t)"),
+            )
+
+        def project(v):
+            n, half = divmod(v, 2)
+            first, second = 2 * half, 2 * half + 1
+            for i in (first, second):
+                result = out_pool.tile([P, WIDTH], F32, name="result")
+                for s in range(2):
+                    acc = for_vector.tile([P, BLOCK], F32, name="bank")
+                    mx_product(acc, yx[n], i * P, wo[s])
+                    if i == first or s == 0:
+                        nc.scalar.copy(out=result[:, s * BLOCK : (s + 1) * BLOCK], in_=acc[:])
+                if i == first:
+                    nc.sync.dma_start(out=out_rows[n][:, i, :], in_=result[:])
+            return {"bank": acc, "result": result, "rows": out_rows[n][:, second, :]}
+
+        def finish(left):
+            nc.vector.tensor_copy(out=left["result"][:, BLOCK:], in_=left["bank"][:])
+            nc.sync.dma_start(out=left["rows"], in_=left["result"][:])
+
+        first_rows = [wq_rows[0], wq_rows[1]] + [q_rows[n] for n in range(EARLY_CHUNKS)]
+        den_nat = []
+        first_nat = []
+        for k in range(CHUNKS):
+            den_nat.append([])
+            first_nat.append([])
+            for h in range(HALVES):
+                den_nat[k].append(load(den_rows[k][h]))
+                first_nat[k].append(load(first_rows[k][h]))
+        wo_nat = [load_block(wo_rows[s]) for s in range(2)]
+        num_nat = [load_block(num_rows[n]) for n in range(CHUNKS)]
+        late_nat = [load_block(q_rows[n]) for n in range(EARLY_CHUNKS, CHUNKS)]
+
+        wq = [mx_tiles("wq%d" % g) for g in range(PASSES)]
+        qx = [mx_tiles("q%d" % n) for n in range(CHUNKS)]
+        wo = [mx_tiles("wo%d" % s) for s in range(2)]
+        yx = [mx_tiles("y%d" % n) for n in range(CHUNKS)]
+        ratio = [keep.tile([P, BLOCK, PACK], F32, name="ratio%d" % u) for u in range(UNITS)]
+
+        early = wq + qx[:EARLY_CHUNKS] + wo
+        early_nat = first_nat + wo_nat
+        waiting = None
+        for k in range(len(early)):
+            grouped = new_grouped()
+            for h in range(HALVES):
+                if k < CHUNKS:
+                    log_denominator(den_nat[k][h], k, h)
+                regroup(early_nat[k][h], grouped, h, False)
+            if waiting is not None:
+                quantise(waiting, early[k - 1])
+            waiting = grouped
+        quantise(waiting, early[len(early) - 1])
+        for u in range(UNITS):
+            nc.scalar.activation(out=ratio[u][:], in_=ratio[u][:], func=ACT.Exp, scale=-1.0)
+
+        sig = {0: gate(0)}
+        y = {}
+        late_grouped = {}
+        for u in range(RATIO_AHEAD):
+            ratio_unit(u)
+        for r in range(UNITS + PROJECT_BEHIND):
+            left = None
+            if r >= PROJECT_BEHIND:
+                left = project(r - PROJECT_BEHIND)
+            if r + 1 < UNITS:
+                sig[r + 1] = gate(r + 1)
+            late, h = divmod(r, HALVES)
+            if late < CHUNKS - EARLY_CHUNKS:
+                if h == 0:
+                    late_grouped[late] = new_grouped()
+                regroup(late_nat[late][h], late_grouped[late], h, True)
+            if 1 <= r <= UNITS:
+                quantise_y(r - 1, y[r - 1])
+            if r < UNITS:
+                y[r] = blend(r, sig[r])
+            if left is not None:
+                finish(left)
+            if h == 0 and 1 <= late <= CHUNKS - EARLY_CHUNKS:
+                quantise(late_grouped[late - 1], qx[EARLY_CHUNKS + late - 1])
+            if r + RATIO_AHEAD < UNITS:
+                ratio_unit(r + RATIO_AHEAD)

@@ -84,11 +84,13 @@ def tile_aftfull_pb_kernel(tc, q, num, den, Wq, Wo, out):
             return bank
 
         def as_values(bank):
-            return bank[:].bitcast(BF16).rearrange("p u (r e) -> p r u e", e=2)
+            return bank[:].bitcast(BF16).rearrange("p u (r e) -> p u e r", e=2)
 
         def part_of(unit_tile, h):
-            rows = unit_tile[:, h * PAIR : (h + 1) * PAIR, :]
-            return rows.rearrange("p r (u e) -> p r u e", e=2)
+            return unit_tile[:, :, h * PAIR : (h + 1) * PAIR].rearrange("p (u e) r -> p u e r", e=2)
+
+        def by_fours(planes):
+            return planes[:].rearrange("p t (c i) -> p c t i", i=4)
 
         def new_grouped():
             return grouped_pool.tile([P, PASSES, BLOCK, PACK], BF16, name="grouped", align_bytes=64)
@@ -149,7 +151,9 @@ def tile_aftfull_pb_kernel(tc, q, num, den, Wq, Wo, out):
 
         def blend(u, sig):
             y = y_pool.tile([P, BLOCK, PACK], BF16, name="y", align_bytes=64)
-            nc.vector.tensor_tensor(out=y[:], in0=sig[:].rearrange("p t r -> p r t"), in1=ratio[u][:], op=MULT)
+            nc.vector.tensor_tensor(
+                out=y[:].rearrange("p (c i) t -> p c t i", i=4), in0=by_fours(sig), in1=by_fours(ratio[u]), op=MULT
+            )
             return y
 
         def quantise_y(u, y):
@@ -196,7 +200,7 @@ def tile_aftfull_pb_kernel(tc, q, num, den, Wq, Wo, out):
         qx = [mx_tiles("q%d" % n) for n in range(CHUNKS)]
         wo = [mx_tiles("wo%d" % s) for s in range(2)]
         yx = [mx_tiles("y%d" % n) for n in range(CHUNKS)]
-        ratio = [keep.tile([P, BLOCK, PACK], F32, name="ratio%d" % u) for u in range(UNITS)]
+        ratio = [keep.tile([P, PACK, BLOCK], F32, name="ratio%d" % u) for u in range(UNITS)]
 
         early = wq + qx[:EARLY_CHUNKS] + wo
         early_nat = first_nat + wo_nat

@@ -24,7 +24,11 @@ CHUNKS = TOKENS // BLOCK
 UNITS = CHUNKS * PASSES
 EARLY_CHUNKS = 2
 PROJECT_BEHIND = 3
-RATIO_AHEAD = 7
+RECIPROCALS_EARLY = 3
+LEAD = 3
+RATIO_AHEAD = 2
+
+RAISE = 2.0**30
 
 FLOPS = 2 * 2 * TOKENS * WIDTH * WIDTH
 
@@ -48,9 +52,8 @@ def tile_aftfull_pb_kernel(tc, q, num, den, Wq, Wo, out):
         keep = ctx.enter_context(tc.tile_pool(name="keep", bufs=1))
         sig_pool = ctx.enter_context(tc.tile_pool(name="sig", bufs=3))
         y_pool = ctx.enter_context(tc.tile_pool(name="y", bufs=2))
-        out_pool = ctx.enter_context(tc.tile_pool(name="outs", bufs=4))
-        for_scalar = ctx.enter_context(tc.psum_pool(name="for_scalar", bufs=4))
-        for_vector = ctx.enter_context(tc.psum_pool(name="for_vector", bufs=4))
+        out_pool = ctx.enter_context(tc.tile_pool(name="outs", bufs=6))
+        banks_pool = ctx.enter_context(tc.psum_pool(name="banks", bufs=8))
 
         ident = const.tile([P, P], F32, name="ident")
         make_identity(nc, ident[:])
@@ -96,7 +99,7 @@ def tile_aftfull_pb_kernel(tc, q, num, den, Wq, Wo, out):
             return grouped_pool.tile([P, PASSES, BLOCK, PACK], BF16, name="grouped", align_bytes=64)
 
         def regroup(nat, grouped, h, on_scalar):
-            banks = [turn(nat, c, for_scalar if on_scalar else for_vector) for c in range(PASSES)]
+            banks = [turn(nat, c, banks_pool) for c in range(PASSES)]
             for c in range(PASSES):
                 side_by_side = grouped[:].bitcast(F32)[:, c, h * PAIR : (h + 1) * PAIR, :]
                 planes = banks[c][:].rearrange("p u r -> p r u")
@@ -113,15 +116,18 @@ def tile_aftfull_pb_kernel(tc, q, num, den, Wq, Wo, out):
             )
 
         def log_denominator(nat, n, h):
-            banks = [turn(nat, g, for_scalar) for g in range(PASSES)]
+            banks = [turn(nat, g, banks_pool) for g in range(PASSES)]
             for g in range(PASSES):
                 nc.scalar.activation(
-                    out=part_of(ratio[PASSES * n + g], h), in_=as_values(banks[g]), func=ACT.Ln
+                    out=part_of(ratio[PASSES * n + g], h), in_=as_values(banks[g]), func=ACT.Ln, scale=RAISE, bias=-1.0
                 )
+
+        def reciprocal(u):
+            nc.scalar.activation(out=ratio[u][:], in_=ratio[u][:], func=ACT.Sigmoid, scale=-1.0)
 
         def ratio_unit(u):
             n, g = divmod(u, PASSES)
-            banks = [turn(num_nat[n][h], g, for_vector) for h in range(HALVES)]
+            banks = [turn(num_nat[n][h], g, banks_pool) for h in range(HALVES)]
             for h in range(HALVES):
                 part = part_of(ratio[u], h)
                 nc.vector.tensor_tensor(out=part, in0=as_values(banks[h]), in1=part, op=MULT)
@@ -144,7 +150,7 @@ def tile_aftfull_pb_kernel(tc, q, num, den, Wq, Wo, out):
             n, g = divmod(u, PASSES)
             sig = sig_pool.tile([P, PACK, BLOCK], F32, name="sig")
             for t in range(PACK):
-                acc = for_scalar.tile([P, BLOCK], F32, name="bank")
+                acc = banks_pool.tile([P, BLOCK], F32, name="bank")
                 mx_product(acc, wq[g], t * P, qx[n])
                 nc.scalar.activation(out=sig[:, t, :], in_=acc[:], func=ACT.Sigmoid)
             return sig
@@ -171,16 +177,20 @@ def tile_aftfull_pb_kernel(tc, q, num, den, Wq, Wo, out):
             for i in (first, second):
                 result = out_pool.tile([P, WIDTH], F32, name="result")
                 for s in range(2):
-                    acc = for_vector.tile([P, BLOCK], F32, name="bank")
+                    acc = banks_pool.tile([P, BLOCK], F32, name="bank")
                     mx_product(acc, yx[n], i * P, wo[s])
                     if i == first or s == 0:
-                        nc.scalar.copy(out=result[:, s * BLOCK : (s + 1) * BLOCK], in_=acc[:])
+                        nc.scalar.activation(
+                            out=result[:, s * BLOCK : (s + 1) * BLOCK], in_=acc[:], func=ACT.Copy, scale=RAISE
+                        )
                 if i == first:
                     nc.sync.dma_start(out=out_rows[n][:, i, :], in_=result[:])
             return {"bank": acc, "result": result, "rows": out_rows[n][:, second, :]}
 
         def finish(left):
-            nc.vector.tensor_copy(out=left["result"][:, BLOCK:], in_=left["bank"][:])
+            nc.vector.tensor_scalar(
+                out=left["result"][:, BLOCK:], in0=left["bank"][:], scalar1=RAISE, scalar2=None, op0=MULT
+            )
             nc.sync.dma_start(out=left["rows"], in_=left["result"][:])
 
         first_rows = [wq_rows[0], wq_rows[1]] + [q_rows[n] for n in range(EARLY_CHUNKS)]
@@ -215,8 +225,8 @@ def tile_aftfull_pb_kernel(tc, q, num, den, Wq, Wo, out):
                 quantise(waiting, early[k - 1])
             waiting = grouped
         quantise(waiting, early[len(early) - 1])
-        for u in range(UNITS):
-            nc.scalar.activation(out=ratio[u][:], in_=ratio[u][:], func=ACT.Exp, scale=-1.0)
+        for u in range(RECIPROCALS_EARLY):
+            reciprocal(u)
 
         sig = {0: gate(0)}
         y = {}
@@ -229,6 +239,8 @@ def tile_aftfull_pb_kernel(tc, q, num, den, Wq, Wo, out):
                 left = project(r - PROJECT_BEHIND)
             if r + 1 < UNITS:
                 sig[r + 1] = gate(r + 1)
+            if RECIPROCALS_EARLY <= r + LEAD < UNITS:
+                reciprocal(r + LEAD)
             late, h = divmod(r, HALVES)
             if late < CHUNKS - EARLY_CHUNKS:
                 if h == 0:

@@ -24,6 +24,9 @@ CHUNKS = TOKENS // BLOCK
 UNITS = CHUNKS * PASSES
 EARLY_CHUNKS = 2
 PROJECT_BEHIND = 3
+GPSIMD_UNITS = ()
+GPSIMD_PIECES = 4
+SCALAR_THREE = (0, 1, 2, 3, 4, 5, 6, 7)
 RECIPROCALS_EARLY = 3
 LEAD = 3
 RATIO_AHEAD = 2
@@ -93,7 +96,7 @@ def tile_aftfull_pb_kernel(tc, q, num, den, Wq, Wo, out):
             return unit_tile[:, :, h * PAIR : (h + 1) * PAIR].rearrange("p (u e) r -> p u e r", e=2)
 
         def by_fours(planes):
-            return planes[:].rearrange("p t (c i) -> p c t i", i=4)
+            return planes.rearrange("p t (c i) -> p c t i", i=4)
 
         def new_grouped():
             return grouped_pool.tile([P, PASSES, BLOCK, PACK], BF16, name="grouped", align_bytes=64)
@@ -157,9 +160,16 @@ def tile_aftfull_pb_kernel(tc, q, num, den, Wq, Wo, out):
 
         def blend(u, sig):
             y = y_pool.tile([P, BLOCK, PACK], BF16, name="y", align_bytes=64)
-            nc.vector.tensor_tensor(
-                out=y[:].rearrange("p (c i) t -> p c t i", i=4), in0=by_fours(sig), in1=by_fours(ratio[u]), op=MULT
-            )
+            pieces = GPSIMD_PIECES if u in GPSIMD_UNITS else 1
+            engine = nc.gpsimd if u in GPSIMD_UNITS else nc.vector
+            for k in range(pieces):
+                rows = slice(k * BLOCK // pieces, (k + 1) * BLOCK // pieces)
+                engine.tensor_tensor(
+                    out=y[:, rows].rearrange("p (c i) t -> p c t i", i=4),
+                    in0=by_fours(sig[:, :, rows]),
+                    in1=by_fours(ratio[u][:, :, rows]),
+                    op=MULT,
+                )
             return y
 
         def quantise_y(u, y):
@@ -173,25 +183,26 @@ def tile_aftfull_pb_kernel(tc, q, num, den, Wq, Wo, out):
 
         def project(v):
             n, half = divmod(v, 2)
-            first, second = 2 * half, 2 * half + 1
-            for i in (first, second):
+            left = []
+            for j in range(2):
+                i = 2 * half + j
                 result = out_pool.tile([P, WIDTH], F32, name="result")
                 for s in range(2):
                     acc = banks_pool.tile([P, BLOCK], F32, name="bank")
                     mx_product(acc, yx[n], i * P, wo[s])
-                    if i == first or s == 0:
-                        nc.scalar.activation(
-                            out=result[:, s * BLOCK : (s + 1) * BLOCK], in_=acc[:], func=ACT.Copy, scale=RAISE
-                        )
-                if i == first:
-                    nc.sync.dma_start(out=out_rows[n][:, i, :], in_=result[:])
-            return {"bank": acc, "result": result, "rows": out_rows[n][:, second, :]}
+                    to = result[:, s * BLOCK : (s + 1) * BLOCK]
+                    rows = out_rows[n][:, i, s * BLOCK : (s + 1) * BLOCK]
+                    if s == 0 or j == 0 or v in (4,):
+                        nc.scalar.activation(out=to, in_=acc[:], func=ACT.Copy, scale=RAISE)
+                        nc.sync.dma_start(out=rows, in_=to)
+                    else:
+                        left.append({"bank": acc, "to": to, "rows": rows})
+            return left
 
         def finish(left):
-            nc.vector.tensor_scalar(
-                out=left["result"][:, BLOCK:], in0=left["bank"][:], scalar1=RAISE, scalar2=None, op0=MULT
-            )
-            nc.sync.dma_start(out=left["rows"], in_=left["result"][:])
+            for item in left:
+                nc.vector.tensor_scalar(out=item["to"], in0=item["bank"][:], scalar1=RAISE, scalar2=None, op0=MULT)
+                nc.sync.dma_start(out=item["rows"], in_=item["to"])
 
         first_rows = [wq_rows[0], wq_rows[1]] + [q_rows[n] for n in range(EARLY_CHUNKS)]
         den_nat = []
@@ -252,6 +263,7 @@ def tile_aftfull_pb_kernel(tc, q, num, den, Wq, Wo, out):
                 y[r] = blend(r, sig[r])
             if left is not None:
                 finish(left)
+            late, h = divmod(r, HALVES)
             if h == 0 and 1 <= late <= CHUNKS - EARLY_CHUNKS:
                 quantise(late_grouped[late - 1], qx[EARLY_CHUNKS + late - 1])
             if r + RATIO_AHEAD < UNITS:

@@ -24,6 +24,7 @@ CHUNKS = TOKENS // BLOCK
 UNITS = CHUNKS * PASSES
 EARLY_CHUNKS = 2
 PROJECT_BEHIND = 3
+RUN = 8
 GPSIMD_UNITS = ()
 GPSIMD_PIECES = 4
 SCALAR_THREE = (0, 1, 2, 3, 4, 5, 6, 7)
@@ -96,7 +97,7 @@ def tile_aftfull_pb_kernel(tc, q, num, den, Wq, Wo, out):
             return unit_tile[:, :, h * PAIR : (h + 1) * PAIR].rearrange("p (u e) r -> p u e r", e=2)
 
         def by_fours(planes):
-            return planes.rearrange("p t (c i) -> p c t i", i=4)
+            return planes.rearrange("p t (c i) -> p c t i", i=RUN)
 
         def new_grouped():
             return grouped_pool.tile([P, PASSES, BLOCK, PACK], BF16, name="grouped", align_bytes=64)
@@ -165,7 +166,7 @@ def tile_aftfull_pb_kernel(tc, q, num, den, Wq, Wo, out):
             for k in range(pieces):
                 rows = slice(k * BLOCK // pieces, (k + 1) * BLOCK // pieces)
                 engine.tensor_tensor(
-                    out=y[:, rows].rearrange("p (c i) t -> p c t i", i=4),
+                    out=y[:, rows].rearrange("p (c i) t -> p c t i", i=RUN),
                     in0=by_fours(sig[:, :, rows]),
                     in1=by_fours(ratio[u][:, :, rows]),
                     op=MULT,

@@ -23,15 +23,10 @@ TOKENS = 2048
 CHUNKS = TOKENS // BLOCK
 UNITS = CHUNKS * PASSES
 EARLY_CHUNKS = 2
+RECIPROCAL_AHEAD = 3
+RATIO_AHEAD = 2
 PROJECT_BEHIND = 3
 RUN = 8
-GPSIMD_UNITS = ()
-GPSIMD_PIECES = 4
-SCALAR_THREE = (0, 1, 2, 3, 4, 5, 6, 7)
-RECIPROCALS_EARLY = 3
-LEAD = 3
-RATIO_AHEAD = 2
-
 RAISE = 2.0**30
 
 FLOPS = 2 * 2 * TOKENS * WIDTH * WIDTH
@@ -41,12 +36,12 @@ def tile_aftfull_pb_kernel(tc, q, num, den, Wq, Wo, out):
     nc = tc.nc
 
     by_token = "(n p h j) k -> n h p (j k)"
-    q_rows = q.flatten_outer_dims().rearrange(by_token, p=P, h=HALVES, j=2).unsqueeze(3)
-    num_rows = num.flatten_outer_dims().rearrange(by_token, p=P, h=HALVES, j=2).unsqueeze(3)
-    den_rows = den.flatten_outer_dims().rearrange(by_token, p=P, h=HALVES, j=2).unsqueeze(3)
+    q_rows = q.flatten_outer_dims().rearrange(by_token, p=P, h=HALVES, j=2)
+    num_rows = num.flatten_outer_dims().rearrange(by_token, p=P, h=HALVES, j=2)
+    den_rows = den.flatten_outer_dims().rearrange(by_token, p=P, h=HALVES, j=2)
     out_rows = out.flatten_outer_dims().rearrange("(n p i) o -> n p i o", p=P, i=2 * HALVES)
-    wq_rows = Wq.rearrange("(g p u e) k -> g u p (e k)", u=HALVES, p=P, e=2).unsqueeze(3)
-    wo_rows = Wo.rearrange("(s h j p) k -> s h p j k", h=HALVES, j=2, p=P)
+    wq_rows = Wq.rearrange("(g p u e) k -> g u p (e k)", u=HALVES, p=P, e=2)
+    wo_rows = Wo.rearrange("(s h p j) k -> s h p (j k)", h=HALVES, p=P, j=2)
 
     with ExitStack() as ctx:
         ctx.enter_context(tc.manual_schedule())
@@ -57,15 +52,14 @@ def tile_aftfull_pb_kernel(tc, q, num, den, Wq, Wo, out):
         sig_pool = ctx.enter_context(tc.tile_pool(name="sig", bufs=3))
         y_pool = ctx.enter_context(tc.tile_pool(name="y", bufs=2))
         out_pool = ctx.enter_context(tc.tile_pool(name="outs", bufs=6))
-        banks_pool = ctx.enter_context(tc.psum_pool(name="banks", bufs=8))
+        psum = ctx.enter_context(tc.psum_pool(name="psum", bufs=8))
 
         ident = const.tile([P, P], F32, name="ident")
         make_identity(nc, ident[:])
 
         def load(rows):
             nat = nat_pool.tile([P, 2, WIDTH], BF16, name="nat")
-            runs = rows.shape[1]
-            nc.sync.dma_start(out=nat[:].rearrange("p (a b) k -> p a (b k)", a=runs), in_=rows)
+            nc.sync.dma_start(out=nat[:].rearrange("p j k -> p (j k)"), in_=rows)
             return nat
 
         def load_block(rows):
@@ -77,9 +71,9 @@ def tile_aftfull_pb_kernel(tc, q, num, den, Wq, Wo, out):
                 "scales": keep.tile([P, PASSES * BLOCK], U8, name=name + "_scales", align_bytes=64),
             }
 
-        def turn(nat, c, pool):
+        def turn(nat, c):
             words = nat[:].bitcast(F32)
-            bank = pool.tile([P, 2, PAIR], F32, name="bank")
+            bank = psum.tile([P, 2, PAIR], F32, name="bank")
             for u in range(2):
                 for j in range(2):
                     first = 2 * c * P + u
@@ -96,21 +90,21 @@ def tile_aftfull_pb_kernel(tc, q, num, den, Wq, Wo, out):
         def part_of(unit_tile, h):
             return unit_tile[:, :, h * PAIR : (h + 1) * PAIR].rearrange("p (u e) r -> p u e r", e=2)
 
-        def by_fours(planes):
-            return planes.rearrange("p t (c i) -> p c t i", i=RUN)
+        def by_runs(slots):
+            return slots.rearrange("p t (c i) -> p c t i", i=RUN)
 
         def new_grouped():
             return grouped_pool.tile([P, PASSES, BLOCK, PACK], BF16, name="grouped", align_bytes=64)
 
         def regroup(nat, grouped, h, on_scalar):
-            banks = [turn(nat, c, banks_pool) for c in range(PASSES)]
+            banks = [turn(nat, c) for c in range(PASSES)]
             for c in range(PASSES):
                 side_by_side = grouped[:].bitcast(F32)[:, c, h * PAIR : (h + 1) * PAIR, :]
-                planes = banks[c][:].rearrange("p u r -> p r u")
+                words = banks[c][:].rearrange("p u r -> p r u")
                 if on_scalar:
-                    nc.scalar.copy(out=side_by_side, in_=planes)
+                    nc.scalar.copy(out=side_by_side, in_=words)
                 else:
-                    nc.vector.tensor_copy(out=side_by_side, in_=planes)
+                    nc.vector.tensor_copy(out=side_by_side, in_=words)
 
         def quantise(grouped, operand):
             nc.vector.quantize_mx(
@@ -120,18 +114,22 @@ def tile_aftfull_pb_kernel(tc, q, num, den, Wq, Wo, out):
             )
 
         def log_denominator(nat, n, h):
-            banks = [turn(nat, g, banks_pool) for g in range(PASSES)]
+            banks = [turn(nat, g) for g in range(PASSES)]
             for g in range(PASSES):
                 nc.scalar.activation(
-                    out=part_of(ratio[PASSES * n + g], h), in_=as_values(banks[g]), func=ACT.Ln, scale=RAISE, bias=-1.0
+                    out=part_of(ratio[PASSES * n + g], h),
+                    in_=as_values(banks[g]),
+                    func=ACT.Ln,
+                    scale=RAISE,
+                    bias=-1.0,
                 )
 
         def reciprocal(u):
             nc.scalar.activation(out=ratio[u][:], in_=ratio[u][:], func=ACT.Sigmoid, scale=-1.0)
 
-        def ratio_unit(u):
+        def times_numerator(u):
             n, g = divmod(u, PASSES)
-            banks = [turn(num_nat[n][h], g, banks_pool) for h in range(HALVES)]
+            banks = [turn(num_nat[n][h], g) for h in range(HALVES)]
             for h in range(HALVES):
                 part = part_of(ratio[u], h)
                 nc.vector.tensor_tensor(out=part, in0=as_values(banks[h]), in1=part, op=MULT)
@@ -154,33 +152,36 @@ def tile_aftfull_pb_kernel(tc, q, num, den, Wq, Wo, out):
             n, g = divmod(u, PASSES)
             sig = sig_pool.tile([P, PACK, BLOCK], F32, name="sig")
             for t in range(PACK):
-                acc = banks_pool.tile([P, BLOCK], F32, name="bank")
+                acc = psum.tile([P, BLOCK], F32, name="bank")
                 mx_product(acc, wq[g], t * P, qx[n])
                 nc.scalar.activation(out=sig[:, t, :], in_=acc[:], func=ACT.Sigmoid)
             return sig
 
+        def pieces_of(u):
+            count = HALVES if u == UNITS - 1 else 1
+            size = BLOCK // count
+            return [slice(k * size, (k + 1) * size) for k in range(count)]
+
         def blend(u, sig):
             y = y_pool.tile([P, BLOCK, PACK], BF16, name="y", align_bytes=64)
-            pieces = GPSIMD_PIECES if u in GPSIMD_UNITS else 1
-            engine = nc.gpsimd if u in GPSIMD_UNITS else nc.vector
-            for k in range(pieces):
-                rows = slice(k * BLOCK // pieces, (k + 1) * BLOCK // pieces)
-                engine.tensor_tensor(
+            for rows in pieces_of(u):
+                nc.vector.tensor_tensor(
                     out=y[:, rows].rearrange("p (c i) t -> p c t i", i=RUN),
-                    in0=by_fours(sig[:, :, rows]),
-                    in1=by_fours(ratio[u][:, :, rows]),
+                    in0=by_runs(sig[:, :, rows]),
+                    in1=by_runs(ratio[u][:, :, rows]),
                     op=MULT,
                 )
             return y
 
         def quantise_y(u, y):
             n, g = divmod(u, PASSES)
-            cols = slice(g * BLOCK, (g + 1) * BLOCK)
-            nc.vector.quantize_mx(
-                out=yx[n]["codes"][:, cols].bitcast(FP8X4),
-                scales=yx[n]["scales"][:, cols],
-                in_=y[:].rearrange("p r t -> p (r t)"),
-            )
+            for rows in pieces_of(u):
+                cols = slice(g * BLOCK + rows.start, g * BLOCK + rows.stop)
+                nc.vector.quantize_mx(
+                    out=yx[n]["codes"][:, cols].bitcast(FP8X4),
+                    scales=yx[n]["scales"][:, cols],
+                    in_=y[:, rows, :].rearrange("p r t -> p (r t)"),
+                )
 
         def project(v):
             n, half = divmod(v, 2)
@@ -189,21 +190,26 @@ def tile_aftfull_pb_kernel(tc, q, num, den, Wq, Wo, out):
                 i = 2 * half + j
                 result = out_pool.tile([P, WIDTH], F32, name="result")
                 for s in range(2):
-                    acc = banks_pool.tile([P, BLOCK], F32, name="bank")
+                    acc = psum.tile([P, BLOCK], F32, name="bank")
                     mx_product(acc, yx[n], i * P, wo[s])
-                    to = result[:, s * BLOCK : (s + 1) * BLOCK]
-                    rows = out_rows[n][:, i, s * BLOCK : (s + 1) * BLOCK]
-                    if s == 0 or j == 0 or v in (4,):
-                        nc.scalar.activation(out=to, in_=acc[:], func=ACT.Copy, scale=RAISE)
-                        nc.sync.dma_start(out=rows, in_=to)
+                    cols = slice(s * BLOCK, (s + 1) * BLOCK)
+                    copy = {
+                        "to": result[:, cols].rearrange("p (h m e) -> p h m e", h=HALVES, e=2),
+                        "bank": acc[:].rearrange("p (h e m) -> p h m e", h=HALVES, e=2),
+                        "rows": out_rows[n][:, i, cols],
+                        "from": result[:, cols],
+                    }
+                    if (j, s) == (1, 1) and v + PROJECT_BEHIND != UNITS - 1:
+                        left.append(copy)
                     else:
-                        left.append({"bank": acc, "to": to, "rows": rows})
+                        nc.scalar.activation(out=copy["to"], in_=copy["bank"], func=ACT.Copy, scale=RAISE)
+                        nc.sync.dma_start(out=copy["rows"], in_=copy["from"])
             return left
 
         def finish(left):
-            for item in left:
-                nc.vector.tensor_scalar(out=item["to"], in0=item["bank"][:], scalar1=RAISE, scalar2=None, op0=MULT)
-                nc.sync.dma_start(out=item["rows"], in_=item["to"])
+            for copy in left:
+                nc.vector.tensor_scalar(out=copy["to"], in0=copy["bank"], scalar1=RAISE, scalar2=None, op0=MULT)
+                nc.sync.dma_start(out=copy["rows"], in_=copy["from"])
 
         first_rows = [wq_rows[0], wq_rows[1]] + [q_rows[n] for n in range(EARLY_CHUNKS)]
         den_nat = []
@@ -215,8 +221,12 @@ def tile_aftfull_pb_kernel(tc, q, num, den, Wq, Wo, out):
                 den_nat[k].append(load(den_rows[k][h]))
                 first_nat[k].append(load(first_rows[k][h]))
         wo_nat = [load_block(wo_rows[s]) for s in range(2)]
-        num_nat = [load_block(num_rows[n]) for n in range(CHUNKS)]
-        late_nat = [load_block(q_rows[n]) for n in range(EARLY_CHUNKS, CHUNKS)]
+        num_nat = [load_block(num_rows[0])]
+        late_nat = []
+        for n in range(1, CHUNKS):
+            if EARLY_CHUNKS + n - 1 < CHUNKS:
+                late_nat.append(load_block(q_rows[EARLY_CHUNKS + n - 1]))
+            num_nat.append(load_block(num_rows[n]))
 
         wq = [mx_tiles("wq%d" % g) for g in range(PASSES)]
         qx = [mx_tiles("q%d" % n) for n in range(CHUNKS)]
@@ -237,22 +247,22 @@ def tile_aftfull_pb_kernel(tc, q, num, den, Wq, Wo, out):
                 quantise(waiting, early[k - 1])
             waiting = grouped
         quantise(waiting, early[len(early) - 1])
-        for u in range(RECIPROCALS_EARLY):
+        for u in range(RECIPROCAL_AHEAD):
             reciprocal(u)
 
         sig = {0: gate(0)}
         y = {}
         late_grouped = {}
         for u in range(RATIO_AHEAD):
-            ratio_unit(u)
+            times_numerator(u)
         for r in range(UNITS + PROJECT_BEHIND):
-            left = None
+            left = []
             if r >= PROJECT_BEHIND:
                 left = project(r - PROJECT_BEHIND)
             if r + 1 < UNITS:
                 sig[r + 1] = gate(r + 1)
-            if RECIPROCALS_EARLY <= r + LEAD < UNITS:
-                reciprocal(r + LEAD)
+            if r + RECIPROCAL_AHEAD < UNITS:
+                reciprocal(r + RECIPROCAL_AHEAD)
             late, h = divmod(r, HALVES)
             if late < CHUNKS - EARLY_CHUNKS:
                 if h == 0:
@@ -262,10 +272,8 @@ def tile_aftfull_pb_kernel(tc, q, num, den, Wq, Wo, out):
                 quantise_y(r - 1, y[r - 1])
             if r < UNITS:
                 y[r] = blend(r, sig[r])
-            if left is not None:
-                finish(left)
-            late, h = divmod(r, HALVES)
+            finish(left)
             if h == 0 and 1 <= late <= CHUNKS - EARLY_CHUNKS:
                 quantise(late_grouped[late - 1], qx[EARLY_CHUNKS + late - 1])
             if r + RATIO_AHEAD < UNITS:
-                ratio_unit(r + RATIO_AHEAD)
+                times_numerator(r + RATIO_AHEAD)

@@ -23,18 +23,19 @@ TOKENS = 2048
 CHUNKS = TOKENS // BLOCK
 UNITS = CHUNKS * PASSES
 EARLY_CHUNKS = 2
-RECIPROCAL_AHEAD = 3
-RATIO_AHEAD = 2
+RECIP_AHEAD = 2
 PROJECT_BEHIND = 3
 RUN = 8
 RAISE = 2.0**30
+LN_ROUND = 2
+LN_FIRST = 4
+S_COPIES = 1
 
 FLOPS = 2 * 2 * TOKENS * WIDTH * WIDTH
 
 
 def tile_aftfull_pb_kernel(tc, q, num, den, Wq, Wo, out):
     nc = tc.nc
-
     by_token = "(n p h j) k -> n h p (j k)"
     q_rows = q.flatten_outer_dims().rearrange(by_token, p=P, h=HALVES, j=2)
     num_rows = num.flatten_outer_dims().rearrange(by_token, p=P, h=HALVES, j=2)
@@ -46,13 +47,15 @@ def tile_aftfull_pb_kernel(tc, q, num, den, Wq, Wo, out):
     with ExitStack() as ctx:
         ctx.enter_context(tc.manual_schedule())
         const = ctx.enter_context(tc.tile_pool(name="const", bufs=1))
-        nat_pool = ctx.enter_context(tc.tile_pool(name="nat", bufs=10))
+        nat_pool = ctx.enter_context(tc.tile_pool(name="nat", bufs=12))
         grouped_pool = ctx.enter_context(tc.tile_pool(name="grouped", bufs=2))
         keep = ctx.enter_context(tc.tile_pool(name="keep", bufs=1))
+        ratio_pool = ctx.enter_context(tc.tile_pool(name="ratio", bufs=6))
         sig_pool = ctx.enter_context(tc.tile_pool(name="sig", bufs=3))
         y_pool = ctx.enter_context(tc.tile_pool(name="y", bufs=2))
         out_pool = ctx.enter_context(tc.tile_pool(name="outs", bufs=6))
-        psum = ctx.enter_context(tc.psum_pool(name="psum", bufs=8))
+        psum = ctx.enter_context(tc.psum_pool(name="psum", bufs=4))
+        gate_psum = ctx.enter_context(tc.psum_pool(name="gates", bufs=4))
 
         ident = const.tile([P, P], F32, name="ident")
         make_identity(nc, ident[:])
@@ -61,9 +64,6 @@ def tile_aftfull_pb_kernel(tc, q, num, den, Wq, Wo, out):
             nat = nat_pool.tile([P, 2, WIDTH], BF16, name="nat")
             nc.sync.dma_start(out=nat[:].rearrange("p j k -> p (j k)"), in_=rows)
             return nat
-
-        def load_block(rows):
-            return [load(rows[h]) for h in range(HALVES)]
 
         def mx_tiles(name):
             return {
@@ -83,12 +83,6 @@ def tile_aftfull_pb_kernel(tc, q, num, den, Wq, Wo, out):
                         identity=ident[:],
                     )
             return bank
-
-        def as_values(bank):
-            return bank[:].bitcast(BF16).rearrange("p u (r e) -> p u e r", e=2)
-
-        def part_of(unit_tile, h):
-            return unit_tile[:, :, h * PAIR : (h + 1) * PAIR].rearrange("p (u e) r -> p u e r", e=2)
 
         def by_runs(slots):
             return slots.rearrange("p t (c i) -> p c t i", i=RUN)
@@ -113,26 +107,45 @@ def tile_aftfull_pb_kernel(tc, q, num, den, Wq, Wo, out):
                 in_=grouped[:].rearrange("p c r t -> p (c r t)"),
             )
 
-        def log_denominator(nat, n, h):
-            banks = [turn(nat, g) for g in range(PASSES)]
-            for g in range(PASSES):
-                nc.scalar.activation(
-                    out=part_of(ratio[PASSES * n + g], h),
-                    in_=as_values(banks[g]),
-                    func=ACT.Ln,
-                    scale=RAISE,
-                    bias=-1.0,
-                )
+        ratio = {}
+
+        def in_slots(nat):
+            return nat[:].rearrange("p j (g m t) -> p (j g) t m", g=PASSES, t=PACK)
+
+        def log_denominator(k):
+            ratio[k] = ratio_pool.tile([P, 2, PASSES, PACK, P], F32, name="ratio")
+            nc.scalar.activation(
+                out=ratio[k][:].rearrange("p j g t m -> p (j g) t m"),
+                in_=in_slots(den_nat[k]),
+                func=ACT.Ln,
+                scale=RAISE,
+                bias=-1.0,
+            )
 
         def reciprocal(u):
-            nc.scalar.activation(out=ratio[u][:], in_=ratio[u][:], func=ACT.Sigmoid, scale=-1.0)
+            n, g = divmod(u, PASSES)
+            for h in range(HALVES):
+                part = ratio[2 * n + h][:, :, g].rearrange("p j t m -> p j (t m)")
+                nc.scalar.activation(out=part, in_=part, func=ACT.Sigmoid, scale=-1.0)
 
         def times_numerator(u):
             n, g = divmod(u, PASSES)
-            banks = [turn(num_nat[n][h], g) for h in range(HALVES)]
             for h in range(HALVES):
-                part = part_of(ratio[u], h)
-                nc.vector.tensor_tensor(out=part, in0=as_values(banks[h]), in1=part, op=MULT)
+                for j in range(2):
+                    part = ratio[2 * n + h][:, j, g]
+                    values = num_nat[2 * n + h][:, j, g * K_PASS : (g + 1) * K_PASS].rearrange("p (m t) -> p t m", t=PACK)
+                    nc.gpsimd.tensor_tensor(out=part, in0=values, in1=part, op=MULT)
+
+        def turn_ratio(u):
+            n, g = divmod(u, PASSES)
+            banks = []
+            for h in range(HALVES):
+                for j in range(2):
+                    bank = psum.tile([P, PACK, P], F32, name="bank")
+                    for t in range(PACK):
+                        nc.tensor.transpose(out=bank[:, t, :], in_=ratio[2 * n + h][:, j, g, t, :], identity=ident[:])
+                    banks.append(bank)
+            return banks
 
         def mx_product(acc, stationary, s_col, moving):
             for c in range(PASSES):
@@ -152,40 +165,36 @@ def tile_aftfull_pb_kernel(tc, q, num, den, Wq, Wo, out):
             n, g = divmod(u, PASSES)
             sig = sig_pool.tile([P, PACK, BLOCK], F32, name="sig")
             for t in range(PACK):
-                acc = psum.tile([P, BLOCK], F32, name="bank")
+                acc = gate_psum.tile([P, BLOCK], F32, name="gbank")
                 mx_product(acc, wq[g], t * P, qx[n])
                 nc.scalar.activation(out=sig[:, t, :], in_=acc[:], func=ACT.Sigmoid)
             return sig
 
-        def pieces_of(u):
-            count = HALVES if u == UNITS - 1 else 1
-            size = BLOCK // count
-            return [slice(k * size, (k + 1) * size) for k in range(count)]
-
-        def blend(u, sig):
+        def blend(u, sig, banks):
             y = y_pool.tile([P, BLOCK, PACK], BF16, name="y", align_bytes=64)
-            for rows in pieces_of(u):
+            for b in range(len(banks)):
+                rows = slice(b * P, (b + 1) * P)
                 nc.vector.tensor_tensor(
                     out=y[:, rows].rearrange("p (c i) t -> p c t i", i=RUN),
-                    in0=by_runs(sig[:, :, rows]),
-                    in1=by_runs(ratio[u][:, :, rows]),
+                    in0=by_runs(banks[b][:]),
+                    in1=by_runs(sig[:, :, rows]),
                     op=MULT,
                 )
             return y
 
         def quantise_y(u, y):
             n, g = divmod(u, PASSES)
-            for rows in pieces_of(u):
-                cols = slice(g * BLOCK + rows.start, g * BLOCK + rows.stop)
-                nc.vector.quantize_mx(
-                    out=yx[n]["codes"][:, cols].bitcast(FP8X4),
-                    scales=yx[n]["scales"][:, cols],
-                    in_=y[:, rows, :].rearrange("p r t -> p (r t)"),
-                )
+            cols = slice(g * BLOCK, (g + 1) * BLOCK)
+            nc.vector.quantize_mx(
+                out=yx[n]["codes"][:, cols].bitcast(FP8X4),
+                scales=yx[n]["scales"][:, cols],
+                in_=y[:].rearrange("p r t -> p (r t)"),
+            )
 
-        def project(v):
+        def project(v, on_scalar):
             n, half = divmod(v, 2)
             left = []
+            k = 0
             for j in range(2):
                 i = 2 * half + j
                 result = out_pool.tile([P, WIDTH], F32, name="result")
@@ -199,11 +208,12 @@ def tile_aftfull_pb_kernel(tc, q, num, den, Wq, Wo, out):
                         "rows": out_rows[n][:, i, cols],
                         "from": result[:, cols],
                     }
-                    if (j, s) == (1, 1) and v + PROJECT_BEHIND != UNITS - 1:
+                    if k >= on_scalar:
                         left.append(copy)
                     else:
                         nc.scalar.activation(out=copy["to"], in_=copy["bank"], func=ACT.Copy, scale=RAISE)
                         nc.sync.dma_start(out=copy["rows"], in_=copy["from"])
+                    k += 1
             return left
 
         def finish(left):
@@ -211,69 +221,94 @@ def tile_aftfull_pb_kernel(tc, q, num, den, Wq, Wo, out):
                 nc.vector.tensor_scalar(out=copy["to"], in0=copy["bank"], scalar1=RAISE, scalar2=None, op0=MULT)
                 nc.sync.dma_start(out=copy["rows"], in_=copy["from"])
 
-        first_rows = [wq_rows[0], wq_rows[1]] + [q_rows[n] for n in range(EARLY_CHUNKS)]
-        den_nat = []
-        first_nat = []
-        for k in range(CHUNKS):
-            den_nat.append([])
-            first_nat.append([])
-            for h in range(HALVES):
-                den_nat[k].append(load(den_rows[k][h]))
-                first_nat[k].append(load(first_rows[k][h]))
-        wo_nat = [load_block(wo_rows[s]) for s in range(2)]
-        num_nat = [load_block(num_rows[0])]
-        late_nat = []
-        for n in range(1, CHUNKS):
-            if EARLY_CHUNKS + n - 1 < CHUNKS:
-                late_nat.append(load_block(q_rows[EARLY_CHUNKS + n - 1]))
-            num_nat.append(load_block(num_rows[n]))
+        den_nat, num_nat, q_nat = {}, {}, {}
+
+        def load_den(k): den_nat[k] = load(den_rows[k // 2][k % 2])
+        def load_num(k): num_nat[k] = load(num_rows[k // 2][k % 2])
+        def load_q(k): q_nat[k] = load(q_rows[k // 2][k % 2])
+
+        wq_nat = [[None] * 2 for g in range(2)]
+        wo_nat = [[None] * 2 for g in range(2)]
+        load_den(0)
+        wq_nat[0][0] = load(wq_rows[0][0])
+        load_den(1)
+        wq_nat[0][1] = load(wq_rows[0][1])
+        load_den(2)
+        load_q(0)
+        load_den(3)
+        load_q(1)
+        wq_nat[1][0] = load(wq_rows[1][0])
+        wq_nat[1][1] = load(wq_rows[1][1])
+        load_num(0)
+        load_num(1)
+        load_q(2)
+        load_q(3)
+        wo_nat = [[load(wo_rows[s][h]) for h in range(2)] for s in range(2)]
+        load_num(2)
+        load_num(3)
+        for k in range(4, 8):
+            load_q(k)
+            load_den(k)
+        for k in range(4, 8):
+            load_num(k)
 
         wq = [mx_tiles("wq%d" % g) for g in range(PASSES)]
         qx = [mx_tiles("q%d" % n) for n in range(CHUNKS)]
         wo = [mx_tiles("wo%d" % s) for s in range(2)]
         yx = [mx_tiles("y%d" % n) for n in range(CHUNKS)]
-        ratio = [keep.tile([P, PACK, BLOCK], F32, name="ratio%d" % u) for u in range(UNITS)]
 
-        early = wq + qx[:EARLY_CHUNKS] + wo
-        early_nat = first_nat + wo_nat
-        waiting = None
-        for k in range(len(early)):
+        def block(nats):
             grouped = new_grouped()
             for h in range(HALVES):
-                if k < CHUNKS:
-                    log_denominator(den_nat[k][h], k, h)
-                regroup(early_nat[k][h], grouped, h, False)
-            if waiting is not None:
-                quantise(waiting, early[k - 1])
-            waiting = grouped
-        quantise(waiting, early[len(early) - 1])
-        for u in range(RECIPROCAL_AHEAD):
-            reciprocal(u)
+                regroup(nats[h], grouped, h, False)
+            return grouped
 
+        for k in range(LN_FIRST):
+            log_denominator(k)
+        waiting = []
+
+        def prepare(nats, op):
+            waiting.append((block(nats), op))
+
+        def flush(keep=0):
+            while len(waiting) > keep:
+                quantise(*waiting.pop(0))
+
+        prepare(wq_nat[0], wq[0])
+        prepare([q_nat[0], q_nat[1]], qx[0])
+        flush()
+        prepare(wq_nat[1], wq[1])
+        reciprocal(0)
+        times_numerator(0)
         sig = {0: gate(0)}
+        flush()
+        prepare([q_nat[2], q_nat[3]], qx[1])
+        flush()
+        reciprocal(1)
+        times_numerator(1)
+        EXTRA = {0: [(wo_nat[0], wo[0])], 1: [(wo_nat[1], wo[1])], 2: [([q_nat[4], q_nat[5]], qx[2])], 3: [([q_nat[6], q_nat[7]], qx[3])]}
+        PROJ = {3: [0, 1], 4: [2], 5: [3], 6: [4], 7: [5], 8: [6, 7]}
+        SC = {0: 0, 1: 0, 2: 1, 3: 1, 4: 1, 5: 1, 6: 2, 7: 2}
         y = {}
-        late_grouped = {}
-        for u in range(RATIO_AHEAD):
-            times_numerator(u)
-        for r in range(UNITS + PROJECT_BEHIND):
-            left = []
-            if r >= PROJECT_BEHIND:
-                left = project(r - PROJECT_BEHIND)
+        for r in range(UNITS + 1):
             if r + 1 < UNITS:
                 sig[r + 1] = gate(r + 1)
-            if r + RECIPROCAL_AHEAD < UNITS:
-                reciprocal(r + RECIPROCAL_AHEAD)
-            late, h = divmod(r, HALVES)
-            if late < CHUNKS - EARLY_CHUNKS:
-                if h == 0:
-                    late_grouped[late] = new_grouped()
-                regroup(late_nat[late][h], late_grouped[late], h, True)
-            if 1 <= r <= UNITS:
-                quantise_y(r - 1, y[r - 1])
+            if r == LN_ROUND:
+                for k in range(LN_FIRST, 8):
+                    log_denominator(k)
+            if r + RECIP_AHEAD < UNITS:
+                reciprocal(r + RECIP_AHEAD)
+                times_numerator(r + RECIP_AHEAD)
             if r < UNITS:
-                y[r] = blend(r, sig[r])
-            finish(left)
-            if h == 0 and 1 <= late <= CHUNKS - EARLY_CHUNKS:
-                quantise(late_grouped[late - 1], qx[EARLY_CHUNKS + late - 1])
-            if r + RATIO_AHEAD < UNITS:
-                times_numerator(r + RATIO_AHEAD)
+                banks = turn_ratio(r)
+                y[r] = blend(r, sig[r], banks)
+            flush()
+            for nats, op in EXTRA.get(r, []):
+                prepare(nats, op)
+                flush(1)
+            if r < UNITS:
+                quantise_y(r, y[r])
+            flush()
+            for v in PROJ.get(r, []):
+                left = project(v, SC[v])
+                finish(left)

@@ -22,14 +22,10 @@ HALVES = BLOCK // PAIR
 TOKENS = 2048
 CHUNKS = TOKENS // BLOCK
 UNITS = CHUNKS * PASSES
-EARLY_CHUNKS = 2
-RECIP_AHEAD = 2
-PROJECT_BEHIND = 3
 RUN = 8
 RAISE = 2.0**30
-LN_ROUND = 2
-LN_FIRST = 4
-S_COPIES = 1
+EARLY_HALVES = 4
+LOG_ROUND = 1
 
 FLOPS = 2 * 2 * TOKENS * WIDTH * WIDTH
 
@@ -54,8 +50,7 @@ def tile_aftfull_pb_kernel(tc, q, num, den, Wq, Wo, out):
         sig_pool = ctx.enter_context(tc.tile_pool(name="sig", bufs=3))
         y_pool = ctx.enter_context(tc.tile_pool(name="y", bufs=2))
         out_pool = ctx.enter_context(tc.tile_pool(name="outs", bufs=6))
-        psum = ctx.enter_context(tc.psum_pool(name="psum", bufs=4))
-        gate_psum = ctx.enter_context(tc.psum_pool(name="gates", bufs=4))
+        psum = ctx.enter_context(tc.psum_pool(name="psum", bufs=8))
 
         ident = const.tile([P, P], F32, name="ident")
         make_identity(nc, ident[:])
@@ -107,44 +102,39 @@ def tile_aftfull_pb_kernel(tc, q, num, den, Wq, Wo, out):
                 in_=grouped[:].rearrange("p c r t -> p (c r t)"),
             )
 
-        ratio = {}
+        ratio = [None] * UNITS
 
-        def in_slots(nat):
-            return nat[:].rearrange("p j (g m t) -> p (j g) t m", g=PASSES, t=PACK)
+        def in_slots(nat, g):
+            return nat[:, :, g * K_PASS : (g + 1) * K_PASS].rearrange("p j (m t) -> p j t m", t=PACK)
 
         def log_denominator(k):
-            ratio[k] = ratio_pool.tile([P, 2, PASSES, PACK, P], F32, name="ratio")
-            nc.scalar.activation(
-                out=ratio[k][:].rearrange("p j g t m -> p (j g) t m"),
-                in_=in_slots(den_nat[k]),
-                func=ACT.Ln,
-                scale=RAISE,
-                bias=-1.0,
-            )
+            n, h = divmod(k, HALVES)
+            for g in range(PASSES):
+                u = PASSES * n + g
+                if h == 0:
+                    ratio[u] = ratio_pool.tile([P, HALVES, 2, PACK, P], F32, name="ratio")
+                nc.scalar.activation(out=ratio[u][:, h], in_=in_slots(den_nat[k], g), func=ACT.Ln, scale=RAISE, bias=-1.0)
 
         def reciprocal(u):
-            n, g = divmod(u, PASSES)
             for h in range(HALVES):
-                part = ratio[2 * n + h][:, :, g].rearrange("p j t m -> p j (t m)")
+                part = ratio[u][:, h].rearrange("p j t m -> p (j t m)")
                 nc.scalar.activation(out=part, in_=part, func=ACT.Sigmoid, scale=-1.0)
 
         def times_numerator(u):
             n, g = divmod(u, PASSES)
             for h in range(HALVES):
+                values = in_slots(num_nat[HALVES * n + h], g)
                 for j in range(2):
-                    part = ratio[2 * n + h][:, j, g]
-                    values = num_nat[2 * n + h][:, j, g * K_PASS : (g + 1) * K_PASS].rearrange("p (m t) -> p t m", t=PACK)
-                    nc.gpsimd.tensor_tensor(out=part, in0=values, in1=part, op=MULT)
+                    part = ratio[u][:, h, j]
+                    nc.gpsimd.tensor_tensor(out=part, in0=values[:, j], in1=part, op=MULT)
 
-        def turn_ratio(u):
-            n, g = divmod(u, PASSES)
+        def turn_ratio(u, bs):
             banks = []
-            for h in range(HALVES):
-                for j in range(2):
-                    bank = psum.tile([P, PACK, P], F32, name="bank")
-                    for t in range(PACK):
-                        nc.tensor.transpose(out=bank[:, t, :], in_=ratio[2 * n + h][:, j, g, t, :], identity=ident[:])
-                    banks.append(bank)
+            for b in bs:
+                bank = psum.tile([P, PACK, P], F32, name="bank")
+                for t in range(PACK):
+                    nc.tensor.transpose(out=bank[:, t, :], in_=ratio[u][:, b // 2, b % 2, t, :], identity=ident[:])
+                banks.append(bank)
             return banks
 
         def mx_product(acc, stationary, s_col, moving):
@@ -161,26 +151,30 @@ def tile_aftfull_pb_kernel(tc, q, num, den, Wq, Wo, out):
                     stop=(c == PASSES - 1),
                 )
 
-        def gate(u):
+        def gate(u, ts=range(4)):
             n, g = divmod(u, PASSES)
-            sig = sig_pool.tile([P, PACK, BLOCK], F32, name="sig")
-            for t in range(PACK):
-                acc = gate_psum.tile([P, BLOCK], F32, name="gbank")
+            if 0 in ts:
+                sigs[u] = sig_pool.tile([P, PACK, BLOCK], F32, name="sig")
+            sig = sigs[u]
+            for t in ts:
+                acc = psum.tile([P, BLOCK], F32, name="bank")
                 mx_product(acc, wq[g], t * P, qx[n])
                 nc.scalar.activation(out=sig[:, t, :], in_=acc[:], func=ACT.Sigmoid)
-            return sig
 
-        def blend(u, sig, banks):
-            y = y_pool.tile([P, BLOCK, PACK], BF16, name="y", align_bytes=64)
-            for b in range(len(banks)):
+        sigs = {}
+        y = {}
+
+        def blend(u, bs):
+            if 0 in bs:
+                y[u] = y_pool.tile([P, BLOCK, PACK], BF16, name="y", align_bytes=64)
+            for b, bank in zip(bs, turn_ratio(u, bs)):
                 rows = slice(b * P, (b + 1) * P)
                 nc.vector.tensor_tensor(
-                    out=y[:, rows].rearrange("p (c i) t -> p c t i", i=RUN),
-                    in0=by_runs(banks[b][:]),
-                    in1=by_runs(sig[:, :, rows]),
+                    out=y[u][:, rows].rearrange("p (c i) t -> p c t i", i=RUN),
+                    in0=by_runs(bank[:]),
+                    in1=by_runs(sigs[u][:, :, rows]),
                     op=MULT,
                 )
-            return y
 
         def quantise_y(u, y):
             n, g = divmod(u, PASSES)
@@ -191,35 +185,19 @@ def tile_aftfull_pb_kernel(tc, q, num, den, Wq, Wo, out):
                 in_=y[:].rearrange("p r t -> p (r t)"),
             )
 
-        def project(v, on_scalar):
-            n, half = divmod(v, 2)
-            left = []
-            k = 0
-            for j in range(2):
-                i = 2 * half + j
-                result = out_pool.tile([P, WIDTH], F32, name="result")
-                for s in range(2):
-                    acc = psum.tile([P, BLOCK], F32, name="bank")
-                    mx_product(acc, yx[n], i * P, wo[s])
-                    cols = slice(s * BLOCK, (s + 1) * BLOCK)
-                    copy = {
-                        "to": result[:, cols].rearrange("p (h m e) -> p h m e", h=HALVES, e=2),
-                        "bank": acc[:].rearrange("p (h e m) -> p h m e", h=HALVES, e=2),
-                        "rows": out_rows[n][:, i, cols],
-                        "from": result[:, cols],
-                    }
-                    if k >= on_scalar:
-                        left.append(copy)
-                    else:
-                        nc.scalar.activation(out=copy["to"], in_=copy["bank"], func=ACT.Copy, scale=RAISE)
-                        nc.sync.dma_start(out=copy["rows"], in_=copy["from"])
-                    k += 1
-            return left
-
-        def finish(left):
-            for copy in left:
-                nc.vector.tensor_scalar(out=copy["to"], in0=copy["bank"], scalar1=RAISE, scalar2=None, op0=MULT)
-                nc.sync.dma_start(out=copy["rows"], in_=copy["from"])
+        def project(n, i, engines):
+            result = out_pool.tile([P, WIDTH], F32, name="result")
+            for s in range(2):
+                acc = psum.tile([P, BLOCK], F32, name="bank")
+                mx_product(acc, yx[n], i * P, wo[s])
+                cols = slice(s * BLOCK, (s + 1) * BLOCK)
+                to = result[:, cols].rearrange("p (h m e) -> p h m e", h=HALVES, e=2)
+                bank = acc[:].rearrange("p (h e m) -> p h m e", h=HALVES, e=2)
+                if engines[s] == "S":
+                    nc.scalar.activation(out=to, in_=bank, func=ACT.Copy, scale=RAISE)
+                else:
+                    nc.vector.tensor_scalar(out=to, in0=bank, scalar1=RAISE, scalar2=None, op0=MULT)
+                nc.sync.dma_start(out=out_rows[n][:, i, cols], in_=result[:, cols])
 
         den_nat, num_nat, q_nat = {}, {}, {}
 
@@ -229,23 +207,27 @@ def tile_aftfull_pb_kernel(tc, q, num, den, Wq, Wo, out):
 
         wq_nat = [[None] * 2 for g in range(2)]
         wo_nat = [[None] * 2 for g in range(2)]
-        load_den(0)
-        wq_nat[0][0] = load(wq_rows[0][0])
-        load_den(1)
-        wq_nat[0][1] = load(wq_rows[0][1])
-        load_den(2)
-        load_q(0)
-        load_den(3)
-        load_q(1)
-        wq_nat[1][0] = load(wq_rows[1][0])
-        wq_nat[1][1] = load(wq_rows[1][1])
-        load_num(0)
-        load_num(1)
-        load_q(2)
-        load_q(3)
-        wo_nat = [[load(wo_rows[s][h]) for h in range(2)] for s in range(2)]
-        load_num(2)
-        load_num(3)
+        wq_nat, wo_nat = {}, {}
+
+        def load_wq(k): wq_nat[k] = load(wq_rows[k // 2][k % 2])
+        def load_wo(k): wo_nat[k] = load(wo_rows[k // 2][k % 2])
+
+        for k in range(2):
+            load_den(k)
+            load_wq(k)
+        for k in range(2):
+            load_den(k + 2)
+            load_q(k)
+        for k in range(2):
+            load_wq(k + 2)
+        for k in range(2):
+            load_num(k)
+        for k in range(2):
+            load_q(k + 2)
+        for k in range(4):
+            load_wo(k)
+        for k in range(2):
+            load_num(k + 2)
         for k in range(4, 8):
             load_q(k)
             load_den(k)
@@ -257,58 +239,54 @@ def tile_aftfull_pb_kernel(tc, q, num, den, Wq, Wo, out):
         wo = [mx_tiles("wo%d" % s) for s in range(2)]
         yx = [mx_tiles("y%d" % n) for n in range(CHUNKS)]
 
+        def two(nats, k):
+            return [nats[2 * k], nats[2 * k + 1]]
+
         def block(nats):
             grouped = new_grouped()
             for h in range(HALVES):
                 regroup(nats[h], grouped, h, False)
             return grouped
 
-        for k in range(LN_FIRST):
+        for k in range(EARLY_HALVES):
             log_denominator(k)
-        waiting = []
-
-        def prepare(nats, op):
-            waiting.append((block(nats), op))
-
-        def flush(keep=0):
-            while len(waiting) > keep:
-                quantise(*waiting.pop(0))
-
-        prepare(wq_nat[0], wq[0])
-        prepare([q_nat[0], q_nat[1]], qx[0])
-        flush()
-        prepare(wq_nat[1], wq[1])
+        quantise(block(two(wq_nat, 0)), wq[0])
+        grouped = block(two(q_nat, 0))
         reciprocal(0)
         times_numerator(0)
-        sig = {0: gate(0)}
-        flush()
-        prepare([q_nat[2], q_nat[3]], qx[1])
-        flush()
+        quantise(grouped, qx[0])
+        quantise(block(two(wq_nat, 1)), wq[1])
+        gate(0)
         reciprocal(1)
         times_numerator(1)
-        EXTRA = {0: [(wo_nat[0], wo[0])], 1: [(wo_nat[1], wo[1])], 2: [([q_nat[4], q_nat[5]], qx[2])], 3: [([q_nat[6], q_nat[7]], qx[3])]}
-        PROJ = {3: [0, 1], 4: [2], 5: [3], 6: [4], 7: [5], 8: [6, 7]}
-        SC = {0: 0, 1: 0, 2: 1, 3: 1, 4: 1, 5: 1, 6: 2, 7: 2}
-        y = {}
-        for r in range(UNITS + 1):
-            if r + 1 < UNITS:
-                sig[r + 1] = gate(r + 1)
-            if r == LN_ROUND:
-                for k in range(LN_FIRST, 8):
+        grouped = block(two(q_nat, 1))
+        reciprocal(2)
+        times_numerator(2)
+        gate(1)
+        quantise(grouped, qx[1])
+
+        blocks = [(two(wo_nat, 0), wo[0]), (two(wo_nat, 1), wo[1]), (two(q_nat, 2), qx[2]), (two(q_nat, 3), qx[3])]
+        products = [(n, i) for n in range(CHUNKS) for i in range(2 * HALVES)]
+        gates, ratios = 2, 3
+        for r in range(UNITS):
+            if r < len(blocks):
+                grouped = block(blocks[r][0])
+            blend(r, range(4))
+            if r == LOG_ROUND:
+                for k in range(EARLY_HALVES, HALVES * CHUNKS):
                     log_denominator(k)
-            if r + RECIP_AHEAD < UNITS:
-                reciprocal(r + RECIP_AHEAD)
-                times_numerator(r + RECIP_AHEAD)
-            if r < UNITS:
-                banks = turn_ratio(r)
-                y[r] = blend(r, sig[r], banks)
-            flush()
-            for nats, op in EXTRA.get(r, []):
-                prepare(nats, op)
-                flush(1)
-            if r < UNITS:
-                quantise_y(r, y[r])
-            flush()
-            for v in PROJ.get(r, []):
-                left = project(v, SC[v])
-                finish(left)
+            elif ratios < UNITS:
+                reciprocal(ratios)
+                times_numerator(ratios)
+                ratios += 1
+            if r >= 2:
+                for n, i in products[2 * (r - 2) : 2 * (r - 1)]:
+                    project(n, i, "SS" if n == 2 else "SV" if (n, i) == (1, 3) else "VV")
+            while gates < UNITS and gates <= r + (1 if r in (LOG_ROUND, LOG_ROUND + 1) else 2):
+                gate(gates)
+                gates += 1
+            quantise_y(r, y[r])
+            if r < len(blocks):
+                quantise(grouped, blocks[r][1])
+        for n, i in products[2 * (UNITS - 2) :]:
+            project(n, i, "SV")

@@ -165,24 +165,24 @@ def tile_aftfull_pb_kernel(tc, q, num, den, Wq, Wo, out):
         y = {}
 
         def blend(u, bs):
-            if 0 in bs:
-                y[u] = y_pool.tile([P, BLOCK, PACK], BF16, name="y", align_bytes=64)
+            n, g = divmod(u, PASSES)
+            if g == 0 and 0 in bs:
+                y[n] = y_pool.tile([P, PASSES, BLOCK, PACK], BF16, name="y", align_bytes=64)
             for b, bank in zip(bs, turn_ratio(u, bs)):
                 rows = slice(b * P, (b + 1) * P)
                 nc.vector.tensor_tensor(
-                    out=y[u][:, rows].rearrange("p (c i) t -> p c t i", i=RUN),
+                    out=y[n][:, g, rows].rearrange("p (c i) t -> p c t i", i=RUN),
                     in0=by_runs(bank[:]),
                     in1=by_runs(sigs[u][:, :, rows]),
                     op=MULT,
                 )
 
-        def quantise_y(u, y):
-            n, g = divmod(u, PASSES)
-            cols = slice(g * BLOCK, (g + 1) * BLOCK)
+        def quantise_y(n, g0, g1):
+            cols = slice(g0 * BLOCK, g1 * BLOCK)
             nc.vector.quantize_mx(
                 out=yx[n]["codes"][:, cols].bitcast(FP8X4),
                 scales=yx[n]["scales"][:, cols],
-                in_=y[:].rearrange("p r t -> p (r t)"),
+                in_=y[n][:, g0:g1].rearrange("p g r t -> p (g r t)"),
             )
 
         def project(n, i, engines):
@@ -285,7 +285,11 @@ def tile_aftfull_pb_kernel(tc, q, num, den, Wq, Wo, out):
             while gates < UNITS and gates <= r + (1 if r in (LOG_ROUND, LOG_ROUND + 1) else 2):
                 gate(gates)
                 gates += 1
-            quantise_y(r, y[r])
+            n, g = divmod(r, PASSES)
+            if n == CHUNKS - 1:
+                quantise_y(n, g, g + 1)
+            elif g == 1:
+                quantise_y(n, 0, PASSES)
             if r < len(blocks):
                 quantise(grouped, blocks[r][1])
         for n, i in products[2 * (UNITS - 2) :]:

@@ -124,9 +124,7 @@ def tile_aftfull_pb_kernel(tc, q, num, den, Wq, Wo, out):
             n, g = divmod(u, PASSES)
             for h in range(HALVES):
                 values = in_slots(num_nat[HALVES * n + h], g)
-                for j in range(2):
-                    part = ratio[u][:, h, j]
-                    nc.gpsimd.tensor_tensor(out=part, in0=values[:, j], in1=part, op=MULT)
+                nc.gpsimd.tensor_tensor(out=ratio[u][:, h], in0=values, in1=ratio[u][:, h], op=MULT)
 
         def turn_ratio(u, bs):
             banks = []

@@ -46,7 +46,7 @@ def tile_aftfull_pb_kernel(tc, q, num, den, Wq, Wo, out):
         nat_pool = ctx.enter_context(tc.tile_pool(name="nat", bufs=12))
         grouped_pool = ctx.enter_context(tc.tile_pool(name="grouped", bufs=2))
         keep = ctx.enter_context(tc.tile_pool(name="keep", bufs=1))
-        ratio_pool = ctx.enter_context(tc.tile_pool(name="ratio", bufs=6))
+        ratio_pool = ctx.enter_context(tc.tile_pool(name="ratio", bufs=3))
         sig_pool = ctx.enter_context(tc.tile_pool(name="sig", bufs=3))
         y_pool = ctx.enter_context(tc.tile_pool(name="y", bufs=2))
         out_pool = ctx.enter_context(tc.tile_pool(name="outs", bufs=6))
@@ -103,17 +103,25 @@ def tile_aftfull_pb_kernel(tc, q, num, den, Wq, Wo, out):
             )
 
         ratio = [None] * UNITS
+        chunks = []
 
         def in_slots(nat, g):
             return nat[:, :, g * K_PASS : (g + 1) * K_PASS].rearrange("p j (m t) -> p j t m", t=PACK)
 
         def log_denominator(k):
             n, h = divmod(k, HALVES)
-            for g in range(PASSES):
-                u = PASSES * n + g
-                if h == 0:
-                    ratio[u] = ratio_pool.tile([P, HALVES, 2, PACK, P], F32, name="ratio")
-                nc.scalar.activation(out=ratio[u][:, h], in_=in_slots(den_nat[k], g), func=ACT.Ln, scale=RAISE, bias=-1.0)
+            if h == 0:
+                chunk = ratio_pool.tile([P, PASSES, HALVES, 2, PACK, P], F32, name="ratio")
+                chunks.append(chunk)
+                for g in range(PASSES):
+                    ratio[PASSES * n + g] = chunk[:, g]
+            nc.scalar.activation(
+                out=chunks[n][:, :, h].rearrange("p g j t m -> p j g t m"),
+                in_=den_nat[k][:].rearrange("p j (g m t) -> p j g t m", g=PASSES, t=PACK),
+                func=ACT.Ln,
+                scale=RAISE,
+                bias=-1.0,
+            )
 
         def reciprocal(u):
             for h in range(HALVES):
@@ -283,12 +291,12 @@ def tile_aftfull_pb_kernel(tc, q, num, den, Wq, Wo, out):
             while gates < UNITS and gates <= r + (1 if r in (LOG_ROUND, LOG_ROUND + 1) else 2):
                 gate(gates)
                 gates += 1
+            if r < len(blocks):
+                quantise(grouped, blocks[r][1])
             n, g = divmod(r, PASSES)
             if n == CHUNKS - 1:
                 quantise_y(n, g, g + 1)
             elif g == 1:
                 quantise_y(n, 0, PASSES)
-            if r < len(blocks):
-                quantise(grouped, blocks[r][1])
         for n, i in products[2 * (UNITS - 2) :]:
             project(n, i, "SV")

from contextlib import ExitStack

import concourse.mybir as mybir
from concourse.masks import make_identity

F32 = mybir.dt.float32
BF16 = mybir.dt.bfloat16
U32 = mybir.dt.uint32
U8 = mybir.dt.uint8
FP8X4 = mybir.dt.float8_e4m3fn_x4
ACT = mybir.ActivationFunctionType
MULT = mybir.AluOpType.mult

P = 128
PACK = 4
K_PASS = P * PACK
WIDTH = 1024
PASSES = WIDTH // K_PASS
BLOCK = 512
PAIR = 2 * P
HALVES = BLOCK // PAIR
TOKENS = 2048
CHUNKS = TOKENS // BLOCK
UNITS = CHUNKS * PASSES
RUN = 8
RAISE = 2.0**30
EARLY_HALVES = 4
LOG_ROUND = 1

FLOPS = 2 * 2 * TOKENS * WIDTH * WIDTH


def tile_aftfull_pb_kernel(tc, q, num, den, Wq, Wo, out):
    nc = tc.nc
    by_token = "(n p h j) k -> n h p (j k)"
    q_rows = q.flatten_outer_dims().rearrange(by_token, p=P, h=HALVES, j=2)
    num_rows = num.flatten_outer_dims().rearrange(by_token, p=P, h=HALVES, j=2)
    den_rows = den.flatten_outer_dims().rearrange(by_token, p=P, h=HALVES, j=2)
    out_rows = out.flatten_outer_dims().rearrange("(n p i) o -> n p i o", p=P, i=2 * HALVES)
    wq_rows = Wq.rearrange("(g p u e) k -> g u p (e k)", u=HALVES, p=P, e=2)
    wo_rows = Wo.rearrange("(s h p j) k -> s h p (j k)", h=HALVES, p=P, j=2)

    with ExitStack() as ctx:
        ctx.enter_context(tc.manual_schedule())
        const = ctx.enter_context(tc.tile_pool(name="const", bufs=1))
        nat_pool = ctx.enter_context(tc.tile_pool(name="nat", bufs=12))
        grouped_pool = ctx.enter_context(tc.tile_pool(name="grouped", bufs=2))
        keep = ctx.enter_context(tc.tile_pool(name="keep", bufs=1))
        ratio_pool = ctx.enter_context(tc.tile_pool(name="ratio", bufs=3))
        sig_pool = ctx.enter_context(tc.tile_pool(name="sig", bufs=3))
        y_pool = ctx.enter_context(tc.tile_pool(name="y", bufs=2))
        out_pool = ctx.enter_context(tc.tile_pool(name="outs", bufs=6))
        psum = ctx.enter_context(tc.psum_pool(name="psum", bufs=8))

        ident = const.tile([P, P], F32, name="ident")
        make_identity(nc, ident[:])

        def load(rows):
            nat = nat_pool.tile([P, 2, WIDTH], BF16, name="nat")
            nc.sync.dma_start(out=nat[:].rearrange("p j k -> p (j k)"), in_=rows)
            return nat

        def mx_tiles(name):
            return {
                "codes": keep.tile([P, PASSES * BLOCK], U32, name=name + "_codes", align_bytes=64),
                "scales": keep.tile([P, PASSES * BLOCK], U8, name=name + "_scales", align_bytes=64),
            }

        def turn(nat, c):
            words = nat[:].bitcast(F32)
            bank = psum.tile([P, 2, PAIR], F32, name="bank")
            for u in range(2):
                for j in range(2):
                    first = 2 * c * P + u
                    nc.tensor.transpose(
                        out=bank[:, u, j * P : (j + 1) * P],
                        in_=words[:, j, first : 2 * (c + 1) * P : 2],
                        identity=ident[:],
                    )
            return bank

        def by_runs(slots):
            return slots.rearrange("p t (c i) -> p c t i", i=RUN)

        def new_grouped():
            return grouped_pool.tile([P, PASSES, BLOCK, PACK], BF16, name="grouped", align_bytes=64)

        def regroup(nat, grouped, h, on_scalar):
            banks = [turn(nat, c) for c in range(PASSES)]
            for c in range(PASSES):
                side_by_side = grouped[:].bitcast(F32)[:, c, h * PAIR : (h + 1) * PAIR, :]
                words = banks[c][:].rearrange("p u r -> p r u")
                if on_scalar:
                    nc.scalar.copy(out=side_by_side, in_=words)
                else:
                    nc.vector.tensor_copy(out=side_by_side, in_=words)

        def quantise(grouped, operand):
            nc.vector.quantize_mx(
                out=operand["codes"][:].bitcast(FP8X4),
                scales=operand["scales"][:],
                in_=grouped[:].rearrange("p c r t -> p (c r t)"),
            )

        ratio = [None] * UNITS
        chunks = []

        def in_slots(nat, g):
            return nat[:, :, g * K_PASS : (g + 1) * K_PASS].rearrange("p j (m t) -> p j t m", t=PACK)

        def log_denominator(k):
            n, h = divmod(k, HALVES)
            if h == 0:
                chunk = ratio_pool.tile([P, PASSES, HALVES, 2, PACK, P], F32, name="ratio")
                chunks.append(chunk)
                for g in range(PASSES):
                    ratio[PASSES * n + g] = chunk[:, g]
            nc.scalar.activation(
                out=chunks[n][:, :, h].rearrange("p g j t m -> p j g t m"),
                in_=den_nat[k][:].rearrange("p j (g m t) -> p j g t m", g=PASSES, t=PACK),
                func=ACT.Ln,
                scale=RAISE,
                bias=-1.0,
            )

        def reciprocal(u):
            for h in range(HALVES):
                part = ratio[u][:, h].rearrange("p j t m -> p (j t m)")
                nc.scalar.activation(out=part, in_=part, func=ACT.Sigmoid, scale=-1.0)

        def times_numerator(u):
            n, g = divmod(u, PASSES)
            for h in range(HALVES):
                values = in_slots(num_nat[HALVES * n + h], g)
                nc.gpsimd.tensor_tensor(out=ratio[u][:, h], in0=values, in1=ratio[u][:, h], op=MULT)

        def turn_ratio(u, bs):
            banks = []
            for b in bs:
                bank = psum.tile([P, PACK, P], F32, name="bank")
                for t in range(PACK):
                    nc.tensor.transpose(out=bank[:, t, :], in_=ratio[u][:, b // 2, b % 2, t, :], identity=ident[:])
                banks.append(bank)
            return banks

        def mx_product(acc, stationary, s_col, moving):
            for c in range(PASSES):
                s_cols = slice(c * BLOCK + s_col, c * BLOCK + s_col + P)
                m_cols = slice(c * BLOCK, (c + 1) * BLOCK)
                nc.tensor.matmul_mx(
                    out=acc[:],
                    lhsT=stationary["codes"][:, s_cols].bitcast(FP8X4),
                    lhsT_scale=stationary["scales"][:, s_cols],
                    rhs=moving["codes"][:, m_cols].bitcast(FP8X4),
                    rhs_scale=moving["scales"][:, m_cols],
                    start=(c == 0),
                    stop=(c == PASSES - 1),
                )

        def gate(u, ts=range(4)):
            n, g = divmod(u, PASSES)
            if 0 in ts:
                sigs[u] = sig_pool.tile([P, PACK, BLOCK], F32, name="sig")
            sig = sigs[u]
            for t in ts:
                acc = psum.tile([P, BLOCK], F32, name="bank")
                mx_product(acc, wq[g], t * P, qx[n])
                nc.scalar.activation(out=sig[:, t, :], in_=acc[:], func=ACT.Sigmoid)

        sigs = {}
        y = {}

        def blend(u, bs):
            n, g = divmod(u, PASSES)
            if g == 0 and 0 in bs:
                y[n] = y_pool.tile([P, PASSES, BLOCK, PACK], BF16, name="y", align_bytes=64)
            for b, bank in zip(bs, turn_ratio(u, bs)):
                rows = slice(b * P, (b + 1) * P)
                nc.vector.tensor_tensor(
                    out=y[n][:, g, rows].rearrange("p (c i) t -> p c t i", i=RUN),
                    in0=by_runs(bank[:]),
                    in1=by_runs(sigs[u][:, :, rows]),
                    op=MULT,
                )

        def quantise_y(n, g0, g1):
            cols = slice(g0 * BLOCK, g1 * BLOCK)
            nc.vector.quantize_mx(
                out=yx[n]["codes"][:, cols].bitcast(FP8X4),
                scales=yx[n]["scales"][:, cols],
                in_=y[n][:, g0:g1].rearrange("p g r t -> p (g r t)"),
            )

        def project(n, i, engines):
            result = out_pool.tile([P, WIDTH], F32, name="result")
            for s in range(2):
                acc = psum.tile([P, BLOCK], F32, name="bank")
                mx_product(acc, yx[n], i * P, wo[s])
                cols = slice(s * BLOCK, (s + 1) * BLOCK)
                to = result[:, cols].rearrange("p (h m e) -> p h m e", h=HALVES, e=2)
                bank = acc[:].rearrange("p (h e m) -> p h m e", h=HALVES, e=2)
                if engines[s] == "S":
                    nc.scalar.activation(out=to, in_=bank, func=ACT.Copy, scale=RAISE)
                else:
                    nc.vector.tensor_scalar(out=to, in0=bank, scalar1=RAISE, scalar2=None, op0=MULT)
                nc.sync.dma_start(out=out_rows[n][:, i, cols], in_=result[:, cols])

        den_nat, num_nat, q_nat = {}, {}, {}

        def load_den(k): den_nat[k] = load(den_rows[k // 2][k % 2])
        def load_num(k): num_nat[k] = load(num_rows[k // 2][k % 2])
        def load_q(k): q_nat[k] = load(q_rows[k // 2][k % 2])

        wq_nat = [[None] * 2 for g in range(2)]
        wo_nat = [[None] * 2 for g in range(2)]
        wq_nat, wo_nat = {}, {}

        def load_wq(k): wq_nat[k] = load(wq_rows[k // 2][k % 2])
        def load_wo(k): wo_nat[k] = load(wo_rows[k // 2][k % 2])

        for k in range(2):
            load_den(k)
            load_wq(k)
        for k in range(2):
            load_den(k + 2)
            load_q(k)
        for k in range(2):
            load_wq(k + 2)
        for k in range(2):
            load_num(k)
        for k in range(2):
            load_q(k + 2)
        for k in range(4):
            load_wo(k)
        for k in range(2):
            load_num(k + 2)
        for k in range(4, 8):
            load_q(k)
            load_den(k)
        for k in range(4, 8):
            load_num(k)

        wq = [mx_tiles("wq%d" % g) for g in range(PASSES)]
        qx = [mx_tiles("q%d" % n) for n in range(CHUNKS)]
        wo = [mx_tiles("wo%d" % s) for s in range(2)]
        yx = [mx_tiles("y%d" % n) for n in range(CHUNKS)]

        def two(nats, k):
            return [nats[2 * k], nats[2 * k + 1]]

        def block(nats):
            grouped = new_grouped()
            for h in range(HALVES):
                regroup(nats[h], grouped, h, False)
            return grouped

        for k in range(EARLY_HALVES):
            log_denominator(k)
        quantise(block(two(wq_nat, 0)), wq[0])
        grouped = block(two(q_nat, 0))
        reciprocal(0)
        times_numerator(0)
        quantise(grouped, qx[0])
        quantise(block(two(wq_nat, 1)), wq[1])
        gate(0)
        reciprocal(1)
        times_numerator(1)
        grouped = block(two(q_nat, 1))
        reciprocal(2)
        times_numerator(2)
        gate(1)
        quantise(grouped, qx[1])

        blocks = [(two(wo_nat, 0), wo[0]), (two(wo_nat, 1), wo[1]), (two(q_nat, 2), qx[2]), (two(q_nat, 3), qx[3])]
        products = [(n, i) for n in range(CHUNKS) for i in range(2 * HALVES)]
        gates, ratios = 2, 3
        for r in range(UNITS):
            if r < len(blocks):
                grouped = block(blocks[r][0])
            blend(r, range(4))
            if r == LOG_ROUND:
                for k in range(EARLY_HALVES, HALVES * CHUNKS):
                    log_denominator(k)
            elif ratios < UNITS:
                reciprocal(ratios)
                times_numerator(ratios)
                ratios += 1
            if r >= 2:
                for n, i in products[2 * (r - 2) : 2 * (r - 1)]:
                    project(n, i, "SS" if n == 2 else "SV" if (n, i) == (1, 3) else "VV")
            while gates < UNITS and gates <= r + (1 if r in (LOG_ROUND, LOG_ROUND + 1) else 2):
                gate(gates)
                gates += 1
            if r < len(blocks):
                quantise(grouped, blocks[r][1])
            n, g = divmod(r, PASSES)
            if n == CHUNKS - 1:
                quantise_y(n, g, g + 1)
            elif g == 1:
                quantise_y(n, 0, PASSES)
        for n, i in products[2 * (UNITS - 2) :]:
            project(n, i, "SV")
